import numpy as np
import ml_dtypes


def mxq(x, axis, fmt="e4m3"):
    dtype, down = {"e4m3": (ml_dtypes.float8_e4m3fn, 7), "e5m2": (ml_dtypes.float8_e5m2, 14)}[fmt]
    v = np.moveaxis(np.asarray(x, np.float32).astype(ml_dtypes.bfloat16).astype(np.float64), axis, -1)
    blocks = v.reshape(v.shape[:-1] + (-1, 32))
    amax = np.abs(blocks).max(-1, keepdims=True)
    byte = np.maximum(np.where(amax > 0, np.frexp(amax)[1] - 1 + 127, 0) - down, 1)
    scale = np.exp2(byte - 127.0)
    codes = (blocks / scale).astype(np.float32).astype(dtype).astype(np.float64)
    return np.moveaxis((codes * scale).reshape(v.shape), -1, axis)


WIDE = False


def mx_kscale(k):
    if not WIDE:
        return np.ones(k)
    levels = np.array([10, -10, 5, -5, 0])
    a = np.random.permutation(np.resize(levels, k // 512 * 4)).reshape(k // 512, 4)
    idx = np.arange(k)
    return np.exp2(a[idx // 512, idx % 128 // 32])


BF16 = ml_dtypes.bfloat16


def bf(x):
    return np.asarray(x, np.float32).astype(BF16)


def f64(x):
    return np.asarray(x).astype(np.float64)


E2M1 = np.array([0.0, 0.5, 1.0, 1.5, 2.0, 3.0, 4.0, 6.0, -0.0, -0.5, -1.0, -1.5, -2.0, -3.0, -4.0, -6.0])


def pack_weight(w, fmt):
    k, n = w.shape
    w = f64(bf(w)).reshape(k // 32, 32, n)
    amax = np.abs(w).max(1)
    if fmt == "e4m3":
        byte = np.frexp(amax)[1] - 1 + 127 - 7
    else:
        mant, ex = np.frexp(amax / 6.0)
        byte = np.where(mant > 0.5, ex, ex - 1) + 127
    byte = np.clip(np.where(amax > 0, byte, 1), 1, 254)
    scaled = (w * np.exp2(127.0 - byte)[:, None, :]).reshape(k, n).astype(np.float32)
    by_word = np.ascontiguousarray(scaled.reshape(k // 512, 128, 4, n).transpose(0, 1, 3, 2))
    if fmt == "e4m3":
        words = by_word.astype(ml_dtypes.float8_e4m3fn).view(np.uint8)
    else:
        c = by_word.astype(ml_dtypes.float4_e2m1fn).view(np.uint8) & 0xF
        words = c[..., 0::2] | (c[..., 1::2] << 4)
    return np.ascontiguousarray(words), np.ascontiguousarray(byte.astype(np.uint8).reshape(k // 512, 16, n))


def unpack_weight(words, scales, fmt):
    g, p, n, _ = words.shape
    if fmt == "e4m3":
        vals = np.ascontiguousarray(words).view(ml_dtypes.float8_e4m3fn).astype(np.float64)
    else:
        nib = np.empty((g, p, n, 4), np.uint8)
        nib[..., 0::2] = words & 0xF
        nib[..., 1::2] = words >> 4
        vals = E2M1[nib]
    vals = vals * np.repeat(np.exp2(scales.astype(np.float64) - 127.0), 8, axis=1)[..., None]
    return vals.transpose(0, 1, 3, 2).reshape(g * 512, n)


B, D, H = 128, 5632, 2048


def setup_inputs():
    s = mx_kscale(D)
    h_c1 = bf(np.random.standard_normal((B, H)))
    h_c2 = bf(np.random.standard_normal((B, H)))
    x_t = bf(np.random.standard_normal((B, D)) * s)
    r_param = bf(np.random.uniform(0.1, 1.05, (1, H)))
    theta_param = bf(np.random.uniform(0.0, 2.0 * np.pi, (1, H)))
    w1_words, w1_scales = pack_weight(np.random.standard_normal((D, H)) / np.sqrt(D) / s[:, None], "e4m3")
    w2_words, w2_scales = pack_weight(np.random.standard_normal((D, H)) / np.sqrt(D) / s[:, None], "e4m3")
    return {"h_c1": h_c1,
            "h_c2": h_c2,
            "x_t": x_t,
            "r_param": r_param,
            "theta_param": theta_param,
            "w1_words": w1_words,
            "w1_scales": w1_scales,
            "w2_words": w2_words,
            "w2_scales": w2_scales}


def reference(h_c1, h_c2, x_t, r_param, theta_param, w1_words, w1_scales, w2_words, w2_scales):
    h_c1, h_c2 = f64(h_c1), f64(h_c2)
    r, theta = f64(r_param), f64(theta_param)
    g = r * np.cos(theta)
    phi = r * np.sin(theta)
    norm = np.sqrt(np.maximum(1.0 - r * r, 0.0))
    xq = mxq(f64(x_t), 1, "e4m3")
    w_c1_x = xq @ unpack_weight(w1_words, w1_scales, "e4m3")
    w_c2_x = xq @ unpack_weight(w2_words, w2_scales, "e4m3")
    h_t_c1 = g * h_c1 - phi * h_c2 + norm * w_c1_x
    h_t_c2 = g * h_c2 + phi * h_c1 + norm * w_c2_x
    h_t = np.maximum(np.concatenate((h_t_c1, h_t_c2), axis=-1), 0.0)
    return (h_t_c1, h_t_c2, h_t)

@@ -1,0 +1,245 @@
+from contextlib import ExitStack
+
+import concourse.mybir as mybir
+from concourse.masks import make_identity
+
+FP8X4 = mybir.dt.float8_e4m3fn_x4
+BF16 = mybir.dt.bfloat16
+F32 = mybir.dt.float32
+I32 = mybir.dt.int32
+U32 = mybir.dt.uint32
+U8 = mybir.dt.uint8
+ALU = mybir.AluOpType
+ACT = mybir.ActivationFunctionType
+
+P = 128
+B, D, H = 128, 5632, 2048
+K_PASS = 512
+G = D // K_PASS
+BANK = 512
+W_BUFS = 13
+AHEAD = 8
+TINY = 1e-30
+FLOPS = 2 * B * D * 2 * H
+
+X_SPLIT = (4, 4, 3)
+
+
+def tile_linearrtus_w_kernel(
+    tc, h_c1, h_c2, x_t, r_param, theta_param,
+    w1_words, w1_scales, w2_words, w2_scales, out_0, out_1, out_2,
+):
+    nc = tc.nc
+    words = (w1_words, w2_words)
+    scales = (w1_scales, w2_scales)
+    outs = (out_0, out_1)
+    with ExitStack() as ctx:
+        const = ctx.enter_context(tc.tile_pool(name="const", bufs=1))
+        wpool = ctx.enter_context(tc.tile_pool(name="wpool", bufs=W_BUFS))
+        psum = ctx.enter_context(tc.psum_pool(name="psum", bufs=1))
+        ctx.enter_context(tc.manual_schedule())
+
+        ident = const.tile([P, P], F32, name="ident")
+        ones = const.tile([P, P], BF16, name="ones")
+        rt = const.tile([P, 2 * H], BF16, name="rt")
+        x_sb = [const.tile([P, K_PASS * n], BF16, name="x_sb%d" % i) for i, n in enumerate(X_SPLIT)]
+        grouped = const.tile([P, G * K_PASS], BF16, name="grouped", align_bytes=64)
+        x_codes = const.tile([P, G * P], U32, name="x_codes", align_bytes=64)
+        x_scales = const.tile([P, G * P], U8, name="x_scales", align_bytes=64)
+        planes = const.tile([P, 6, H], U8, name="planes", align_bytes=64)
+        h_sb = [const.tile([P, H], BF16, name="h_sb%d" % i) for i in range(2)]
+        r_sb = const.tile([P, H], BF16, name="r_sb")
+        s2 = const.tile([P, H], F32, name="s2")
+        ph = const.tile([P, H], F32, name="ph")
+        gq = const.tile([P, H], F32, name="gq")
+        nv = const.tile([P, H], F32, name="nv")
+        sq = const.tile([P, H], F32, name="sq")
+        acc_sb = [const.tile([P, H], F32, name="acc_sb%d" % i) for i in range(2)]
+        warm = const.tile([P, 1], F32, name="warm")
+        relu_sb = (gq, ph)
+        tmp = s2
+
+        def bank(i, shape, dtype, name):
+            return psum.tile(shape, dtype, name=name, tag="bank%d" % i)
+
+        nc.vector.memset(warm[:], 0.0)
+        nc.scalar.activation(out=warm[:], in_=warm[:], func=ACT.Sin)
+        nc.vector.memset(rt[:, 0:H].bitcast(I32), 0)
+        nc.gpsimd.memset(rt[:, H:2 * H].bitcast(F32), 0.0)
+        nc.vector.memset(ones[:], 1.0)
+        make_identity(nc, ident[:])
+        nc.sync.dma_start(out=x_sb[0][:], in_=x_t[:, 0:2048])
+        nc.sync.dma_start(out=rt[0:1, 0:H], in_=theta_param[:, :])
+        nc.sync.dma_start(out=rt[0:1, H:2 * H], in_=r_param[:, :])
+        nc.sync.dma_start(out=x_sb[1][:], in_=x_t[:, 2048:4096])
+        nc.sync.dma_start(out=x_sb[2][:], in_=x_t[:, 4096:D])
+        for s in range(6):
+            nc.vector.memset(planes[:, s, :].bitcast(I32), 0)
+
+        grouped_w = grouped[:].bitcast(F32).rearrange("p (g b u) -> p g b u", g=G, b=B, u=2)
+        xt_banks = (0, 1, 2, 3, 0, 1)
+        n_pairs = (G + 1) // 2
+        xts = []
+        spread = []
+
+        def transposes(t):
+            xt = bank(xt_banks[t], [P, 2, 2, B], F32, "xt%d" % t)
+            for gi in range(min(2, G - 2 * t)):
+                g = 2 * t + gi
+                src = x_sb[g // 4][:].bitcast(F32)
+                gl = g % 4
+                for u in range(2):
+                    nc.tensor.transpose(out=xt[:, gi, u, :], in_=src[:, 256 * gl + u:256 * (gl + 1):2],
+                                        identity=ident[:])
+            xts.append(xt)
+
+        def spread_out(i):
+            sp = bank(4 + i, [P, 2 * BANK], BF16, "spread%d" % i)
+            for j in range(2):
+                c0 = 2 * BANK * i + BANK * j
+                nc.tensor.matmul(out=sp[:, BANK * j:BANK * (j + 1)], lhsT=ones[:], rhs=rt[:, c0:c0 + BANK],
+                                 start=True, stop=True)
+            spread.append(sp)
+
+        def regroup(t):
+            n = min(2, G - 2 * t)
+            nc.vector.tensor_copy(out=grouped_w[:, 2 * t:2 * t + n, :, :],
+                                  in_=xts[t][:, 0:n, :, :].rearrange("p g u b -> p g b u"))
+
+        def quantise(t):
+            n = min(2, G - 2 * t)
+            nc.vector.quantize_mx(
+                out=x_codes[:, 256 * t:256 * t + P * n].bitcast(FP8X4),
+                scales=x_scales[:, 256 * t:256 * t + P * n],
+                in_=grouped[:, 1024 * t:1024 * t + K_PASS * n],
+            )
+
+        transposes(0)
+        transposes(1)
+        spread_out(0)
+        spread_out(1)
+        transposes(2)
+        transposes(3)
+        spread_out(2)
+        spread_out(3)
+        regroup(0)
+        regroup(1)
+        quantise(0)
+        transposes(4)
+        transposes(5)
+        for t in range(2, n_pairs):
+            regroup(t)
+            quantise(t - 1)
+        quantise(n_pairs - 1)
+
+        halves = (slice(0, 1024), slice(1024, 2048))
+        for i in range(2):
+            nc.scalar.activation(out=ph[:, halves[i]], in_=spread[i][:], func=ACT.Sin, scale=0.25)
+        nc.scalar.activation(out=ph[:], in_=ph[:], func=ACT.Square)
+        for i in range(2):
+            nc.scalar.activation(out=s2[:, halves[i]], in_=spread[i][:], func=ACT.Sin, scale=0.5)
+        for i in range(2):
+            nc.scalar.copy(out=r_sb[:, halves[i]], in_=spread[2 + i][:])
+        nc.scalar.activation(out=gq[:], in_=s2[:], func=ACT.Square)
+        nc.scalar.activation(out=nv[:], in_=r_sb[:], func=ACT.Square)
+        nc.vector.tensor_scalar(out=ph[:], in0=ph[:], scalar1=-4.0, scalar2=2.0, op0=ALU.mult, op1=ALU.add)
+        nc.vector.tensor_tensor(out=ph[:], in0=ph[:], in1=s2[:], op=ALU.mult)
+        nc.vector.tensor_tensor(out=ph[:], in0=ph[:], in1=r_sb[:], op=ALU.mult)
+        nc.vector.tensor_scalar(out=gq[:], in0=gq[:], scalar1=-2.0, scalar2=1.0, op0=ALU.mult, op1=ALU.add)
+        nc.vector.tensor_tensor(out=gq[:], in0=gq[:], in1=r_sb[:], op=ALU.mult)
+        nc.vector.tensor_scalar(out=nv[:], in0=nv[:], scalar1=-1.0, scalar2=1.0, op0=ALU.mult, op1=ALU.add)
+        nc.vector.tensor_scalar_max(out=sq[:], in0=nv[:], scalar1=TINY)
+        nc.scalar.activation(out=sq[:], in_=sq[:], func=ACT.Sqrt)
+
+        def state_terms():
+            nc.vector.tensor_tensor(out=acc_sb[0][:], in0=h_sb[0][:], in1=gq[:], op=ALU.mult)
+            nc.vector.tensor_tensor(out=tmp[:], in0=h_sb[1][:], in1=ph[:], op=ALU.mult)
+            nc.vector.scalar_tensor_tensor(out=nv[:], in0=nv[:], scalar=0.0, in1=sq[:], op0=ALU.is_gt, op1=ALU.mult)
+            nc.vector.tensor_tensor(out=acc_sb[1][:], in0=h_sb[1][:], in1=gq[:], op=ALU.mult)
+            nc.vector.tensor_tensor(out=sq[:], in0=h_sb[0][:], in1=ph[:], op=ALU.mult)
+            nc.vector.tensor_tensor(out=acc_sb[0][:], in0=acc_sb[0][:], in1=tmp[:], op=ALU.subtract)
+            nc.vector.tensor_tensor(out=acc_sb[1][:], in0=acc_sb[1][:], in1=sq[:], op=ALU.add)
+
+        def load_scales(s):
+            w, g0 = s // 3, 4 * (s % 3)
+            n = min(4, G - g0)
+            for q in (0, 2, 1, 3):
+                nc.sync.dma_start(out=planes[32 * q:32 * q + 4 * n, s, :].bitcast(I32),
+                                  in_=scales[w][g0:g0 + n, 4 * q:4 * q + 4, :].bitcast(I32))
+
+        def load_words(w, gs, c0, ncol):
+            wt = wpool.tile([P, H], U32, name="wt", tag="wt", align_bytes=64)
+            n = len(gs)
+            nc.sync.dma_start(
+                out=wt[:, 0:n * ncol].rearrange("p (g n) -> p g n", g=n).bitcast(I32),
+                in_=words[w][gs[0]:gs[0] + n].rearrange("g p n t -> p g (n t)")[:, :, 4 * c0:4 * (c0 + ncol)].bitcast(I32),
+            )
+            return wt
+
+        accs = {}
+
+        def multiply(w, gs, c0, ncol, wt):
+            for gi, g in enumerate(gs):
+                s, k = 3 * w + g // 4, 4 * (g % 4)
+                for c in range(c0, c0 + ncol, BANK):
+                    if g == 0:
+                        b = c // BANK + 4 * w
+                        accs[(w, c)] = bank(b, [P, BANK], F32, "acc%d" % b)
+                    o = gi * ncol + c - c0
+                    nc.tensor.matmul_mx(
+                        out=accs[(w, c)][:],
+                        lhsT=x_codes[:, P * g:P * (g + 1)].bitcast(FP8X4),
+                        lhsT_scale=x_scales[:, P * g:P * (g + 1)],
+                        rhs=wt[:, o:o + BANK].bitcast(FP8X4),
+                        rhs_scale=planes[k:P, s, c:c + BANK],
+                        start=(g == 0),
+                        stop=(g == G - 1),
+                    )
+
+        def finish(w, c0, ncol):
+            for c in range(c0, c0 + ncol, BANK):
+                cols = slice(c, c + BANK)
+                nc.vector.tensor_tensor(out=tmp[:, cols], in0=accs[(w, c)][:], in1=nv[:, cols], op=ALU.mult)
+                nc.vector.tensor_tensor(out=acc_sb[w][:, cols], in0=acc_sb[w][:, cols], in1=tmp[:, cols], op=ALU.add)
+                nc.scalar.activation(out=relu_sb[w][:, cols], in_=acc_sb[w][:, cols], func=ACT.Relu)
+
+        def store(w, c0, ncol, relu_queue):
+            cols = slice(c0, c0 + ncol)
+            nc.sync.dma_start(out=outs[w][:, cols], in_=acc_sb[w][:, cols])
+            relu_queue.dma_start(out=out_2[:, H * w + c0:H * w + c0 + ncol], in_=relu_sb[w][:, cols])
+
+        stream = []
+        for w in range(2):
+            for g in range(G - w):
+                stream.append((w, (g,), 0, H))
+        for c in range(0, H, BANK):
+            stream.append((1, (G - 1,), c, BANK))
+        extras = {2: (0,), 4: (-1, 1), 8: (2,), 11: (3,), 15: (4,), 19: (5,)}
+        stores = {BANK: (0, 2 * BANK), 2 * BANK: (2 * BANK, BANK), 3 * BANK: (3 * BANK, BANK)}
+
+        tiles = []
+
+        def issue(i):
+            for e in extras.get(i, ()):
+                if e < 0:
+                    nc.sync.dma_start(out=h_sb[0][:], in_=h_c1[:, :])
+                    nc.sync.dma_start(out=h_sb[1][:], in_=h_c2[:, :])
+                    state_terms()
+                else:
+                    load_scales(e)
+            tiles.append(load_words(stream[i][0], stream[i][1], stream[i][2], stream[i][3]))
+
+        n_jobs = len(stream)
+        for i in range(AHEAD):
+            issue(i)
+        for i in range(n_jobs):
+            w, gs, c0, ncol = stream[i]
+            multiply(w, gs, c0, ncol, tiles[i])
+            if gs[-1] == G - 1:
+                finish(w, c0, ncol)
+                if w == 1 and c0 in stores:
+                    store(1, stores[c0][0], stores[c0][1], nc.scalar)
+            if i + AHEAD < n_jobs:
+                issue(i + AHEAD)
+            if i + AHEAD == n_jobs - 1:
+                store(0, 0, H, nc.sync)

@@ -56,6 +56,7 @@ def tile_linearrtus_w_kernel(
         sq = const.tile([P, H], F32, name="sq")
         acc_sb = [const.tile([P, H], F32, name="acc_sb%d" % i) for i in range(2)]
         warm = const.tile([P, 1], F32, name="warm")
+        gate = const.tile([P, 1], F32, name="gate")
         relu_sb = (gq, ph)
         tmp = s2
 
@@ -75,6 +76,13 @@ def tile_linearrtus_w_kernel(
         nc.sync.dma_start(out=x_sb[2][:], in_=x_t[:, 4096:D])
         for s in range(6):
             nc.vector.memset(planes[:, s, :].bitcast(I32), 0)
+        for s in range(6):
+            w, g0 = s // 3, 4 * (s % 3)
+            n = min(4, G - g0)
+            for q in (0, 2, 1, 3):
+                nc.gpsimd.dma_start(out=planes[32 * q:32 * q + 4 * n, s, :].bitcast(F32),
+                                    in_=scales[w][g0:g0 + n, 4 * q:4 * q + 4, :].bitcast(F32))
+        nc.gpsimd.memset(gate[:], TINY)
 
         grouped_w = grouped[:].bitcast(F32).rearrange("p (g b u) -> p g b u", g=G, b=B, u=2)
         xt_banks = (0, 1, 2, 3, 0, 1)
@@ -136,20 +144,20 @@ def tile_linearrtus_w_kernel(
         for i in range(2):
             nc.scalar.activation(out=ph[:, halves[i]], in_=spread[i][:], func=ACT.Sin, scale=0.25)
         nc.scalar.activation(out=ph[:], in_=ph[:], func=ACT.Square)
+        nc.scalar.activation(out=ph[:], in_=ph[:], func=ACT.Copy, scale=-4.0, bias=2.0)
         for i in range(2):
             nc.scalar.activation(out=s2[:, halves[i]], in_=spread[i][:], func=ACT.Sin, scale=0.5)
         for i in range(2):
             nc.scalar.copy(out=r_sb[:, halves[i]], in_=spread[2 + i][:])
-        nc.scalar.activation(out=gq[:], in_=s2[:], func=ACT.Square)
         nc.scalar.activation(out=nv[:], in_=r_sb[:], func=ACT.Square)
-        nc.vector.tensor_scalar(out=ph[:], in0=ph[:], scalar1=-4.0, scalar2=2.0, op0=ALU.mult, op1=ALU.add)
+        nc.scalar.activation(out=nv[:], in_=nv[:], func=ACT.Copy, scale=-1.0, bias=1.0)
+        nc.scalar.activation(out=gq[:], in_=s2[:], func=ACT.Square)
+        nc.scalar.activation(out=gq[:], in_=gq[:], func=ACT.Copy, scale=-2.0, bias=1.0)
+        nc.vector.tensor_scalar(out=sq[:], in0=nv[:], scalar1=gate[:, 0:1], scalar2=None, op0=ALU.max)
+        nc.scalar.activation(out=sq[:], in_=sq[:], func=ACT.Sqrt)
         nc.vector.tensor_tensor(out=ph[:], in0=ph[:], in1=s2[:], op=ALU.mult)
         nc.vector.tensor_tensor(out=ph[:], in0=ph[:], in1=r_sb[:], op=ALU.mult)
-        nc.vector.tensor_scalar(out=gq[:], in0=gq[:], scalar1=-2.0, scalar2=1.0, op0=ALU.mult, op1=ALU.add)
         nc.vector.tensor_tensor(out=gq[:], in0=gq[:], in1=r_sb[:], op=ALU.mult)
-        nc.vector.tensor_scalar(out=nv[:], in0=nv[:], scalar1=-1.0, scalar2=1.0, op0=ALU.mult, op1=ALU.add)
-        nc.vector.tensor_scalar_max(out=sq[:], in0=nv[:], scalar1=TINY)
-        nc.scalar.activation(out=sq[:], in_=sq[:], func=ACT.Sqrt)
 
         def state_terms():
             nc.vector.tensor_tensor(out=acc_sb[0][:], in0=h_sb[0][:], in1=gq[:], op=ALU.mult)
@@ -159,13 +167,6 @@ def tile_linearrtus_w_kernel(
             nc.vector.tensor_tensor(out=sq[:], in0=h_sb[0][:], in1=ph[:], op=ALU.mult)
             nc.vector.tensor_tensor(out=acc_sb[0][:], in0=acc_sb[0][:], in1=tmp[:], op=ALU.subtract)
             nc.vector.tensor_tensor(out=acc_sb[1][:], in0=acc_sb[1][:], in1=sq[:], op=ALU.add)
-
-        def load_scales(s):
-            w, g0 = s // 3, 4 * (s % 3)
-            n = min(4, G - g0)
-            for q in (0, 2, 1, 3):
-                nc.sync.dma_start(out=planes[32 * q:32 * q + 4 * n, s, :].bitcast(I32),
-                                  in_=scales[w][g0:g0 + n, 4 * q:4 * q + 4, :].bitcast(I32))
 
         def load_words(w, gs, c0, ncol):
             wt = wpool.tile([P, H], U32, name="wt", tag="wt", align_bytes=64)
@@ -214,19 +215,16 @@ def tile_linearrtus_w_kernel(
                 stream.append((w, (g,), 0, H))
         for c in range(0, H, BANK):
             stream.append((1, (G - 1,), c, BANK))
-        extras = {2: (0,), 4: (-1, 1), 8: (2,), 11: (3,), 15: (4,), 19: (5,)}
+        H_AT = 4
         stores = {BANK: (0, 2 * BANK), 2 * BANK: (2 * BANK, BANK), 3 * BANK: (3 * BANK, BANK)}
 
         tiles = []
 
         def issue(i):
-            for e in extras.get(i, ()):
-                if e < 0:
-                    nc.sync.dma_start(out=h_sb[0][:], in_=h_c1[:, :])
-                    nc.sync.dma_start(out=h_sb[1][:], in_=h_c2[:, :])
-                    state_terms()
-                else:
-                    load_scales(e)
+            if i == H_AT:
+                nc.sync.dma_start(out=h_sb[0][:], in_=h_c1[:, :])
+                nc.sync.dma_start(out=h_sb[1][:], in_=h_c2[:, :])
+                state_terms()
             tiles.append(load_words(stream[i][0], stream[i][1], stream[i][2], stream[i][3]))
 
         n_jobs = len(stream)

@@ -19,6 +19,7 @@ G = D // K_PASS
 BANK = 512
 W_BUFS = 13
 AHEAD = 8
+LAST = 3
 TINY = 1e-30
 FLOPS = 2 * B * D * 2 * H
 
@@ -70,9 +71,9 @@ def tile_linearrtus_w_kernel(
         nc.vector.memset(ones[:], 1.0)
         make_identity(nc, ident[:])
         nc.sync.dma_start(out=x_sb[0][:], in_=x_t[:, 0:2048])
+        nc.sync.dma_start(out=x_sb[1][:], in_=x_t[:, 2048:4096])
         nc.sync.dma_start(out=rt[0:1, 0:H], in_=theta_param[:, :])
         nc.sync.dma_start(out=rt[0:1, H:2 * H], in_=r_param[:, :])
-        nc.sync.dma_start(out=x_sb[1][:], in_=x_t[:, 2048:4096])
         nc.sync.dma_start(out=x_sb[2][:], in_=x_t[:, 4096:D])
         for s in range(6):
             nc.vector.memset(planes[:, s, :].bitcast(I32), 0)
@@ -210,13 +211,13 @@ def tile_linearrtus_w_kernel(
             relu_queue.dma_start(out=out_2[:, H * w + c0:H * w + c0 + ncol], in_=relu_sb[w][:, cols])
 
         stream = []
-        for w in range(2):
-            for g in range(G - w):
-                stream.append((w, (g,), 0, H))
+        for g in range(G):
+            stream.append((0, (g,), 0, H))
+        for g in range(G - LAST):
+            stream.append((1, (g,), 0, H))
         for c in range(0, H, BANK):
-            stream.append((1, (G - 1,), c, BANK))
+            stream.append((1, tuple(range(G - LAST, G)), c, BANK))
         H_AT = 4
-        stores = {BANK: (0, 2 * BANK), 2 * BANK: (2 * BANK, BANK), 3 * BANK: (3 * BANK, BANK)}
 
         tiles = []
 
@@ -235,8 +236,8 @@ def tile_linearrtus_w_kernel(
             multiply(w, gs, c0, ncol, tiles[i])
             if gs[-1] == G - 1:
                 finish(w, c0, ncol)
-                if w == 1 and c0 in stores:
-                    store(1, stores[c0][0], stores[c0][1], nc.scalar)
+                if w == 1:
+                    store(1, c0, ncol, nc.scalar)
             if i + AHEAD < n_jobs:
                 issue(i + AHEAD)
             if i + AHEAD == n_jobs - 1:

@@ -237,7 +237,7 @@ def tile_linearrtus_w_kernel(
             if gs[-1] == G - 1:
                 finish(w, c0, ncol)
                 if w == 1:
-                    store(1, c0, ncol, nc.scalar)
+                    store(1, c0, ncol, nc.sync)
             if i + AHEAD < n_jobs:
                 issue(i + AHEAD)
             if i + AHEAD == n_jobs - 1:

@@ -66,15 +66,14 @@ def tile_linearrtus_w_kernel(
 
         nc.vector.memset(warm[:], 0.0)
         nc.scalar.activation(out=warm[:], in_=warm[:], func=ACT.Sin)
-        nc.vector.memset(rt[:, 0:H].bitcast(I32), 0)
-        nc.gpsimd.memset(rt[:, H:2 * H].bitcast(F32), 0.0)
+        nc.vector.memset(rt[:].bitcast(I32), 0)
         nc.vector.memset(ones[:], 1.0)
         make_identity(nc, ident[:])
         nc.sync.dma_start(out=x_sb[0][:], in_=x_t[:, 0:2048])
         nc.sync.dma_start(out=x_sb[1][:], in_=x_t[:, 2048:4096])
-        nc.sync.dma_start(out=rt[0:1, 0:H], in_=theta_param[:, :])
-        nc.sync.dma_start(out=rt[0:1, H:2 * H], in_=r_param[:, :])
         nc.sync.dma_start(out=x_sb[2][:], in_=x_t[:, 4096:D])
+        nc.scalar.dma_start(out=rt[0:1, 0:H], in_=theta_param[:, :])
+        nc.scalar.dma_start(out=rt[0:1, H:2 * H], in_=r_param[:, :])
         for s in range(6):
             nc.vector.memset(planes[:, s, :].bitcast(I32), 0)
         for s in range(6):

@@ -13,17 +13,17 @@ ALU = mybir.AluOpType
 ACT = mybir.ActivationFunctionType
 
 P = 128
-B, D, H = 128, 5632, 2048
+D, H = 5632, 2048
 K_PASS = 512
-G = D // K_PASS
+N_PASS = D // K_PASS
 BANK = 512
+SHARE = 4
+N_SETS = (N_PASS + SHARE - 1) // SHARE
 W_BUFS = 13
 AHEAD = 8
 LAST = 3
 TINY = 1e-30
-FLOPS = 2 * B * D * 2 * H
-
-X_SPLIT = (4, 4, 3)
+FLOPS = 2 * P * D * 2 * H
 
 
 def tile_linearrtus_w_kernel(
@@ -31,213 +31,197 @@ def tile_linearrtus_w_kernel(
     w1_words, w1_scales, w2_words, w2_scales, out_0, out_1, out_2,
 ):
     nc = tc.nc
-    words = (w1_words, w2_words)
-    scales = (w1_scales, w2_scales)
+    w_words = (w1_words, w2_words)
+    w_scales = (w1_scales, w2_scales)
     outs = (out_0, out_1)
     with ExitStack() as ctx:
-        const = ctx.enter_context(tc.tile_pool(name="const", bufs=1))
+        keep = ctx.enter_context(tc.tile_pool(name="keep", bufs=1))
         wpool = ctx.enter_context(tc.tile_pool(name="wpool", bufs=W_BUFS))
         psum = ctx.enter_context(tc.psum_pool(name="psum", bufs=1))
         ctx.enter_context(tc.manual_schedule())
 
-        ident = const.tile([P, P], F32, name="ident")
-        ones = const.tile([P, P], BF16, name="ones")
-        rt = const.tile([P, 2 * H], BF16, name="rt")
-        x_sb = [const.tile([P, K_PASS * n], BF16, name="x_sb%d" % i) for i, n in enumerate(X_SPLIT)]
-        grouped = const.tile([P, G * K_PASS], BF16, name="grouped", align_bytes=64)
-        x_codes = const.tile([P, G * P], U32, name="x_codes", align_bytes=64)
-        x_scales = const.tile([P, G * P], U8, name="x_scales", align_bytes=64)
-        planes = const.tile([P, 6, H], U8, name="planes", align_bytes=64)
-        h_sb = [const.tile([P, H], BF16, name="h_sb%d" % i) for i in range(2)]
-        r_sb = const.tile([P, H], BF16, name="r_sb")
-        s2 = const.tile([P, H], F32, name="s2")
-        ph = const.tile([P, H], F32, name="ph")
-        gq = const.tile([P, H], F32, name="gq")
-        nv = const.tile([P, H], F32, name="nv")
-        sq = const.tile([P, H], F32, name="sq")
-        acc_sb = [const.tile([P, H], F32, name="acc_sb%d" % i) for i in range(2)]
-        warm = const.tile([P, 1], F32, name="warm")
-        gate = const.tile([P, 1], F32, name="gate")
-        relu_sb = (gq, ph)
-        tmp = s2
+        def row_tile(name, tag):
+            return keep.tile([P, H], F32, name=name, tag=tag)
 
-        def bank(i, shape, dtype, name):
+        def bank_tile(i, shape, dtype, name):
             return psum.tile(shape, dtype, name=name, tag="bank%d" % i)
 
-        nc.vector.memset(warm[:], 0.0)
-        nc.scalar.activation(out=warm[:], in_=warm[:], func=ACT.Sin)
-        nc.vector.memset(rt[:].bitcast(I32), 0)
+        x_sb = keep.tile([P, D], BF16, name="x_sb")
+        h_sb = [keep.tile([P, H], BF16, name="h_sb%d" % i) for i in range(2)]
+        nc.sync.dma_start(out=x_sb[:], in_=x_t[:, :])
+        nc.sync.dma_start(out=h_sb[0][:], in_=h_c1[:, :])
+        nc.sync.dma_start(out=h_sb[1][:], in_=h_c2[:, :])
+
+        vec_rows = keep.tile([P, 2 * H], BF16, name="vec_rows")
+        ones = keep.tile([P, P], BF16, name="ones")
+        ident = keep.tile([P, P], F32, name="ident")
+        nc.vector.memset(vec_rows[:].bitcast(I32), 0)
         nc.vector.memset(ones[:], 1.0)
         make_identity(nc, ident[:])
-        nc.sync.dma_start(out=x_sb[0][:], in_=x_t[:, 0:2048])
-        nc.sync.dma_start(out=x_sb[1][:], in_=x_t[:, 2048:4096])
-        nc.sync.dma_start(out=x_sb[2][:], in_=x_t[:, 4096:D])
-        nc.scalar.dma_start(out=rt[0:1, 0:H], in_=theta_param[:, :])
-        nc.scalar.dma_start(out=rt[0:1, H:2 * H], in_=r_param[:, :])
-        for s in range(6):
-            nc.vector.memset(planes[:, s, :].bitcast(I32), 0)
-        for s in range(6):
-            w, g0 = s // 3, 4 * (s % 3)
-            n = min(4, G - g0)
-            for q in (0, 2, 1, 3):
-                nc.gpsimd.dma_start(out=planes[32 * q:32 * q + 4 * n, s, :].bitcast(F32),
-                                    in_=scales[w][g0:g0 + n, 4 * q:4 * q + 4, :].bitcast(F32))
-        nc.gpsimd.memset(gate[:], TINY)
+        nc.scalar.dma_start(out=vec_rows[0:1, 0:H], in_=theta_param[:, :])
+        nc.scalar.dma_start(out=vec_rows[0:1, H:2 * H], in_=r_param[:, :])
 
-        grouped_w = grouped[:].bitcast(F32).rearrange("p (g b u) -> p g b u", g=G, b=B, u=2)
-        xt_banks = (0, 1, 2, 3, 0, 1)
-        n_pairs = (G + 1) // 2
-        xts = []
-        spread = []
+        planes = keep.tile([P, 2 * N_SETS, H], U8, name="planes", align_bytes=64)
+        tiny = keep.tile([P, 1], F32, name="tiny")
 
-        def transposes(t):
-            xt = bank(xt_banks[t], [P, 2, 2, B], F32, "xt%d" % t)
-            for gi in range(min(2, G - 2 * t)):
-                g = 2 * t + gi
-                src = x_sb[g // 4][:].bitcast(F32)
-                gl = g % 4
+        def load_scale_rows(w, s):
+            n = min(SHARE, N_PASS - SHARE * s)
+            t = N_SETS * w + s
+            nc.vector.memset(planes[:, t, :].bitcast(I32), 0)
+            for quadrant in range(4):
+                nc.gpsimd.dma_start(
+                    out=planes[32 * quadrant:32 * quadrant + 4 * n, t, :].bitcast(F32),
+                    in_=w_scales[w][SHARE * s:SHARE * s + n, 4 * quadrant:4 * quadrant + 4, :].bitcast(F32),
+                )
+
+        for w in range(2):
+            for s in range(N_SETS):
+                load_scale_rows(w, s)
+        nc.gpsimd.memset(tiny[:], TINY)
+
+        x_words = x_sb[:].bitcast(F32)
+        x_grouped = keep.tile([P, N_PASS * K_PASS], BF16, name="x_grouped", align_bytes=64)
+        x_grouped_words = x_grouped[:].bitcast(F32).rearrange("p (g b u) -> p g b u", g=N_PASS, b=P, u=2)
+        x_codes = keep.tile([P, N_PASS * P], U32, name="x_codes", align_bytes=64)
+        x_scales = keep.tile([P, N_PASS * P], U8, name="x_scales", align_bytes=64)
+        n_pairs = (N_PASS + 1) // 2
+        transposed = []
+
+        def passes_of(pair):
+            return range(2 * pair, min(2 * pair + 2, N_PASS))
+
+        def transpose_pair(pair):
+            xt = bank_tile(pair % 4, [P, 2, 2, P], F32, "xt%d" % pair)
+            for g in passes_of(pair):
                 for u in range(2):
-                    nc.tensor.transpose(out=xt[:, gi, u, :], in_=src[:, 256 * gl + u:256 * (gl + 1):2],
+                    nc.tensor.transpose(out=xt[:, g % 2, u, :], in_=x_words[:, 256 * g + u:256 * (g + 1):2],
                                         identity=ident[:])
-            xts.append(xt)
+            transposed.append(xt)
 
-        def spread_out(i):
-            sp = bank(4 + i, [P, 2 * BANK], BF16, "spread%d" % i)
-            for j in range(2):
-                c0 = 2 * BANK * i + BANK * j
-                nc.tensor.matmul(out=sp[:, BANK * j:BANK * (j + 1)], lhsT=ones[:], rhs=rt[:, c0:c0 + BANK],
-                                 start=True, stop=True)
-            spread.append(sp)
+        def regroup_pair(pair):
+            n = len(passes_of(pair))
+            nc.vector.tensor_copy(out=x_grouped_words[:, 2 * pair:2 * pair + n, :, :],
+                                  in_=transposed[pair][:, 0:n, :, :].rearrange("p g u b -> p g b u"))
 
-        def regroup(t):
-            n = min(2, G - 2 * t)
-            nc.vector.tensor_copy(out=grouped_w[:, 2 * t:2 * t + n, :, :],
-                                  in_=xts[t][:, 0:n, :, :].rearrange("p g u b -> p g b u"))
-
-        def quantise(t):
-            n = min(2, G - 2 * t)
+        def quantise_pair(pair):
+            n = len(passes_of(pair))
             nc.vector.quantize_mx(
-                out=x_codes[:, 256 * t:256 * t + P * n].bitcast(FP8X4),
-                scales=x_scales[:, 256 * t:256 * t + P * n],
-                in_=grouped[:, 1024 * t:1024 * t + K_PASS * n],
+                out=x_codes[:, 2 * P * pair:2 * P * pair + P * n].bitcast(FP8X4),
+                scales=x_scales[:, 2 * P * pair:2 * P * pair + P * n],
+                in_=x_grouped[:, 2 * K_PASS * pair:2 * K_PASS * pair + K_PASS * n],
             )
 
-        transposes(0)
-        transposes(1)
-        spread_out(0)
-        spread_out(1)
-        transposes(2)
-        transposes(3)
-        spread_out(2)
-        spread_out(3)
-        regroup(0)
-        regroup(1)
-        quantise(0)
-        transposes(4)
-        transposes(5)
-        for t in range(2, n_pairs):
-            regroup(t)
-            quantise(t - 1)
-        quantise(n_pairs - 1)
+        def spread(i):
+            out = bank_tile(4 + i, [P, 2 * BANK], BF16, "spread%d" % i)
+            for j in range(2):
+                c = 2 * BANK * i + BANK * j
+                nc.tensor.matmul(out=out[:, BANK * j:BANK * (j + 1)], lhsT=ones[:], rhs=vec_rows[:, c:c + BANK],
+                                 start=True, stop=True)
+            return out
 
-        halves = (slice(0, 1024), slice(1024, 2048))
-        for i in range(2):
-            nc.scalar.activation(out=ph[:, halves[i]], in_=spread[i][:], func=ACT.Sin, scale=0.25)
-        nc.scalar.activation(out=ph[:], in_=ph[:], func=ACT.Square)
-        nc.scalar.activation(out=ph[:], in_=ph[:], func=ACT.Copy, scale=-4.0, bias=2.0)
-        for i in range(2):
-            nc.scalar.activation(out=s2[:, halves[i]], in_=spread[i][:], func=ACT.Sin, scale=0.5)
-        for i in range(2):
-            nc.scalar.copy(out=r_sb[:, halves[i]], in_=spread[2 + i][:])
-        nc.scalar.activation(out=nv[:], in_=r_sb[:], func=ACT.Square)
-        nc.scalar.activation(out=nv[:], in_=nv[:], func=ACT.Copy, scale=-1.0, bias=1.0)
-        nc.scalar.activation(out=gq[:], in_=s2[:], func=ACT.Square)
-        nc.scalar.activation(out=gq[:], in_=gq[:], func=ACT.Copy, scale=-2.0, bias=1.0)
-        nc.vector.tensor_scalar(out=sq[:], in0=nv[:], scalar1=gate[:, 0:1], scalar2=None, op0=ALU.max)
-        nc.scalar.activation(out=sq[:], in_=sq[:], func=ACT.Sqrt)
-        nc.vector.tensor_tensor(out=ph[:], in0=ph[:], in1=s2[:], op=ALU.mult)
-        nc.vector.tensor_tensor(out=ph[:], in0=ph[:], in1=r_sb[:], op=ALU.mult)
-        nc.vector.tensor_tensor(out=gq[:], in0=gq[:], in1=r_sb[:], op=ALU.mult)
+        for pair in range(4):
+            transpose_pair(pair)
+        theta_all = [spread(0), spread(1)]
+        r_psum = [spread(2), spread(3)]
+        for pair in range(n_pairs):
+            regroup_pair(pair)
+            if pair + 4 < n_pairs:
+                transpose_pair(pair + 4)
+            if pair > 0:
+                quantise_pair(pair - 1)
+        quantise_pair(n_pairs - 1)
 
-        def state_terms():
-            nc.vector.tensor_tensor(out=acc_sb[0][:], in0=h_sb[0][:], in1=gq[:], op=ALU.mult)
-            nc.vector.tensor_tensor(out=tmp[:], in0=h_sb[1][:], in1=ph[:], op=ALU.mult)
-            nc.vector.scalar_tensor_tensor(out=nv[:], in0=nv[:], scalar=0.0, in1=sq[:], op0=ALU.is_gt, op1=ALU.mult)
-            nc.vector.tensor_tensor(out=acc_sb[1][:], in0=h_sb[1][:], in1=gq[:], op=ALU.mult)
-            nc.vector.tensor_tensor(out=sq[:], in0=h_sb[0][:], in1=ph[:], op=ALU.mult)
-            nc.vector.tensor_tensor(out=acc_sb[0][:], in0=acc_sb[0][:], in1=tmp[:], op=ALU.subtract)
-            nc.vector.tensor_tensor(out=acc_sb[1][:], in0=acc_sb[1][:], in1=sq[:], op=ALU.add)
+        halves = (slice(0, H // 2), slice(H // 2, H))
+        r_all = keep.tile([P, H], BF16, name="r_all")
+        sin_half = row_tile("sin_half", "a")
+        root = row_tile("root", "b")
+        g_all = row_tile("g_all", "c")
+        phi_all = row_tile("phi_all", "d")
+        norm_all = row_tile("norm_all", "e")
+        for i in range(2):
+            nc.scalar.activation(out=phi_all[:, halves[i]], in_=theta_all[i][:], func=ACT.Sin, scale=0.25)
+        nc.scalar.activation(out=phi_all[:], in_=phi_all[:], func=ACT.Square)
+        nc.scalar.activation(out=phi_all[:], in_=phi_all[:], func=ACT.Copy, scale=-4.0, bias=2.0)
+        for i in range(2):
+            nc.scalar.activation(out=sin_half[:, halves[i]], in_=theta_all[i][:], func=ACT.Sin, scale=0.5)
+        for i in range(2):
+            nc.scalar.copy(out=r_all[:, halves[i]], in_=r_psum[i][:])
+        nc.scalar.activation(out=norm_all[:], in_=r_all[:], func=ACT.Square)
+        nc.scalar.activation(out=norm_all[:], in_=norm_all[:], func=ACT.Copy, scale=-1.0, bias=1.0)
+        nc.scalar.activation(out=g_all[:], in_=sin_half[:], func=ACT.Square)
+        nc.scalar.activation(out=g_all[:], in_=g_all[:], func=ACT.Copy, scale=-2.0, bias=1.0)
+        nc.vector.tensor_scalar(out=root[:], in0=norm_all[:], scalar1=tiny[:, 0:1], scalar2=None, op0=ALU.max)
+        nc.scalar.activation(out=root[:], in_=root[:], func=ACT.Sqrt)
+        nc.vector.tensor_tensor(out=phi_all[:], in0=phi_all[:], in1=sin_half[:], op=ALU.mult)
+        nc.vector.tensor_tensor(out=phi_all[:], in0=phi_all[:], in1=r_all[:], op=ALU.mult)
+        nc.vector.tensor_tensor(out=g_all[:], in0=g_all[:], in1=r_all[:], op=ALU.mult)
 
-        def load_words(w, gs, c0, ncol):
+        result = [row_tile("result0", "f"), row_tile("result1", "g")]
+        nc.vector.tensor_tensor(out=result[0][:], in0=h_sb[0][:], in1=g_all[:], op=ALU.mult)
+        cross0 = row_tile("cross0", "a")
+        nc.vector.tensor_tensor(out=cross0[:], in0=h_sb[1][:], in1=phi_all[:], op=ALU.mult)
+        nc.vector.scalar_tensor_tensor(out=norm_all[:], in0=norm_all[:], scalar=0.0, in1=root[:],
+                                       op0=ALU.is_gt, op1=ALU.mult)
+        nc.vector.tensor_tensor(out=result[1][:], in0=h_sb[1][:], in1=g_all[:], op=ALU.mult)
+        cross1 = row_tile("cross1", "b")
+        nc.vector.tensor_tensor(out=cross1[:], in0=h_sb[0][:], in1=phi_all[:], op=ALU.mult)
+        nc.vector.tensor_tensor(out=result[0][:], in0=result[0][:], in1=cross0[:], op=ALU.subtract)
+        nc.vector.tensor_tensor(out=result[1][:], in0=result[1][:], in1=cross1[:], op=ALU.add)
+        scaled = row_tile("scaled", "a")
+        relu = [row_tile("relu0", "c"), row_tile("relu1", "d")]
+
+        loads = [(0, g, 1, 0, H) for g in range(N_PASS)]
+        loads += [(1, g, 1, 0, H) for g in range(N_PASS - LAST)]
+        loads += [(1, N_PASS - LAST, LAST, c, BANK) for c in range(0, H, BANK)]
+        w_tiles = []
+        sums = {}
+
+        def load(w, g0, n, c0, cols):
             wt = wpool.tile([P, H], U32, name="wt", tag="wt", align_bytes=64)
-            n = len(gs)
             nc.sync.dma_start(
-                out=wt[:, 0:n * ncol].rearrange("p (g n) -> p g n", g=n).bitcast(I32),
-                in_=words[w][gs[0]:gs[0] + n].rearrange("g p n t -> p g (n t)")[:, :, 4 * c0:4 * (c0 + ncol)].bitcast(I32),
+                out=wt[:, 0:n * cols].rearrange("p (g c) -> p g c", g=n).bitcast(I32),
+                in_=w_words[w][g0:g0 + n].rearrange("g p c t -> p g (c t)")[:, :, 4 * c0:4 * (c0 + cols)].bitcast(I32),
             )
-            return wt
+            w_tiles.append(wt)
 
-        accs = {}
-
-        def multiply(w, gs, c0, ncol, wt):
-            for gi, g in enumerate(gs):
-                s, k = 3 * w + g // 4, 4 * (g % 4)
-                for c in range(c0, c0 + ncol, BANK):
+        def multiply(w, g0, n, c0, cols, wt):
+            for g in range(g0, g0 + n):
+                for c in range(c0, c0 + cols, BANK):
                     if g == 0:
-                        b = c // BANK + 4 * w
-                        accs[(w, c)] = bank(b, [P, BANK], F32, "acc%d" % b)
-                    o = gi * ncol + c - c0
+                        b = 4 * w + c // BANK
+                        sums[(w, c)] = bank_tile(b, [P, BANK], F32, "sum%d" % b)
+                    at = (g - g0) * cols + c - c0
                     nc.tensor.matmul_mx(
-                        out=accs[(w, c)][:],
+                        out=sums[(w, c)][:],
                         lhsT=x_codes[:, P * g:P * (g + 1)].bitcast(FP8X4),
                         lhsT_scale=x_scales[:, P * g:P * (g + 1)],
-                        rhs=wt[:, o:o + BANK].bitcast(FP8X4),
-                        rhs_scale=planes[k:P, s, c:c + BANK],
+                        rhs=wt[:, at:at + BANK].bitcast(FP8X4),
+                        rhs_scale=planes[4 * (g % SHARE):P, N_SETS * w + g // SHARE, c:c + BANK],
                         start=(g == 0),
-                        stop=(g == G - 1),
+                        stop=(g == N_PASS - 1),
                     )
 
-        def finish(w, c0, ncol):
-            for c in range(c0, c0 + ncol, BANK):
-                cols = slice(c, c + BANK)
-                nc.vector.tensor_tensor(out=tmp[:, cols], in0=accs[(w, c)][:], in1=nv[:, cols], op=ALU.mult)
-                nc.vector.tensor_tensor(out=acc_sb[w][:, cols], in0=acc_sb[w][:, cols], in1=tmp[:, cols], op=ALU.add)
-                nc.scalar.activation(out=relu_sb[w][:, cols], in_=acc_sb[w][:, cols], func=ACT.Relu)
+        def finish(w, c):
+            at = slice(c, c + BANK)
+            nc.vector.tensor_tensor(out=scaled[:, at], in0=sums[(w, c)][:], in1=norm_all[:, at], op=ALU.mult)
+            nc.vector.tensor_tensor(out=result[w][:, at], in0=result[w][:, at], in1=scaled[:, at], op=ALU.add)
+            nc.scalar.activation(out=relu[w][:, at], in_=result[w][:, at], func=ACT.Relu)
 
-        def store(w, c0, ncol, relu_queue):
-            cols = slice(c0, c0 + ncol)
-            nc.sync.dma_start(out=outs[w][:, cols], in_=acc_sb[w][:, cols])
-            relu_queue.dma_start(out=out_2[:, H * w + c0:H * w + c0 + ncol], in_=relu_sb[w][:, cols])
+        def store(w, c0, cols):
+            nc.sync.dma_start(out=outs[w][:, c0:c0 + cols], in_=result[w][:, c0:c0 + cols])
+            nc.sync.dma_start(out=out_2[:, H * w + c0:H * w + c0 + cols], in_=relu[w][:, c0:c0 + cols])
 
-        stream = []
-        for g in range(G):
-            stream.append((0, (g,), 0, H))
-        for g in range(G - LAST):
-            stream.append((1, (g,), 0, H))
-        for c in range(0, H, BANK):
-            stream.append((1, tuple(range(G - LAST, G)), c, BANK))
-        H_AT = 4
-
-        tiles = []
-
-        def issue(i):
-            if i == H_AT:
-                nc.sync.dma_start(out=h_sb[0][:], in_=h_c1[:, :])
-                nc.sync.dma_start(out=h_sb[1][:], in_=h_c2[:, :])
-                state_terms()
-            tiles.append(load_words(stream[i][0], stream[i][1], stream[i][2], stream[i][3]))
-
-        n_jobs = len(stream)
         for i in range(AHEAD):
-            issue(i)
-        for i in range(n_jobs):
-            w, gs, c0, ncol = stream[i]
-            multiply(w, gs, c0, ncol, tiles[i])
-            if gs[-1] == G - 1:
-                finish(w, c0, ncol)
+            load(*loads[i])
+        for i in range(len(loads)):
+            w, g0, n, c0, cols = loads[i]
+            multiply(w, g0, n, c0, cols, w_tiles[i])
+            if g0 + n == N_PASS:
+                for c in range(c0, c0 + cols, BANK):
+                    finish(w, c)
                 if w == 1:
-                    store(1, c0, ncol, nc.sync)
-            if i + AHEAD < n_jobs:
-                issue(i + AHEAD)
-            if i + AHEAD == n_jobs - 1:
-                store(0, 0, H, nc.sync)
+                    store(1, c0, cols)
+            if i + AHEAD < len(loads):
+                load(*loads[i + AHEAD])
+            if i + AHEAD == len(loads) - 1:
+                store(0, 0, H)

@@ -52,14 +52,8 @@ def tile_linearrtus_w_kernel(
         nc.sync.dma_start(out=h_sb[0][:], in_=h_c1[:, :])
         nc.sync.dma_start(out=h_sb[1][:], in_=h_c2[:, :])
 
-        vec_rows = keep.tile([P, 2 * H], BF16, name="vec_rows")
-        ones = keep.tile([P, P], BF16, name="ones")
         ident = keep.tile([P, P], F32, name="ident")
-        nc.vector.memset(vec_rows[:].bitcast(I32), 0)
-        nc.vector.memset(ones[:], 1.0)
         make_identity(nc, ident[:])
-        nc.scalar.dma_start(out=vec_rows[0:1, 0:H], in_=theta_param[:, :])
-        nc.scalar.dma_start(out=vec_rows[0:1, H:2 * H], in_=r_param[:, :])
 
         planes = keep.tile([P, 2 * N_SETS, H], U8, name="planes", align_bytes=64)
         tiny = keep.tile([P, 1], F32, name="tiny")
@@ -78,6 +72,13 @@ def tile_linearrtus_w_kernel(
             for s in range(N_SETS):
                 load_scale_rows(w, s)
         nc.gpsimd.memset(tiny[:], TINY)
+
+        vec_rows = keep.tile([P, 2 * H], BF16, name="vec_rows")
+        ones = keep.tile([P, P], BF16, name="ones")
+        nc.vector.memset(vec_rows[:].bitcast(I32), 0)
+        nc.vector.memset(ones[:], 1.0)
+        nc.scalar.dma_start(out=vec_rows[0:1, 0:H], in_=theta_param[:, :])
+        nc.scalar.dma_start(out=vec_rows[0:1, H:2 * H], in_=r_param[:, :])
 
         x_words = x_sb[:].bitcast(F32)
         x_grouped = keep.tile([P, N_PASS * K_PASS], BF16, name="x_grouped", align_bytes=64)
@@ -132,29 +133,31 @@ def tile_linearrtus_w_kernel(
         quantise_pair(n_pairs - 1)
 
         halves = (slice(0, H // 2), slice(H // 2, H))
-        r_all = keep.tile([P, H], BF16, name="r_all")
         sin_half = row_tile("sin_half", "a")
         root = row_tile("root", "b")
         g_all = row_tile("g_all", "c")
         phi_all = row_tile("phi_all", "d")
         norm_all = row_tile("norm_all", "e")
         for i in range(2):
+            nc.scalar.activation(out=norm_all[:, halves[i]], in_=r_psum[i][:], func=ACT.Square)
+        nc.scalar.activation(out=norm_all[:], in_=norm_all[:], func=ACT.Copy, scale=-1.0, bias=1.0)
+        for i in range(2):
+            nc.scalar.activation(out=sin_half[:, halves[i]], in_=theta_all[i][:], func=ACT.Sin, scale=0.5)
+        nc.scalar.activation(out=g_all[:], in_=sin_half[:], func=ACT.Square)
+        nc.scalar.activation(out=g_all[:], in_=g_all[:], func=ACT.Copy, scale=-2.0, bias=1.0)
+        for i in range(2):
             nc.scalar.activation(out=phi_all[:, halves[i]], in_=theta_all[i][:], func=ACT.Sin, scale=0.25)
         nc.scalar.activation(out=phi_all[:], in_=phi_all[:], func=ACT.Square)
         nc.scalar.activation(out=phi_all[:], in_=phi_all[:], func=ACT.Copy, scale=-4.0, bias=2.0)
         for i in range(2):
-            nc.scalar.activation(out=sin_half[:, halves[i]], in_=theta_all[i][:], func=ACT.Sin, scale=0.5)
+            nc.vector.tensor_tensor(out=sin_half[:, halves[i]], in0=sin_half[:, halves[i]], in1=r_psum[i][:],
+                                    op=ALU.mult)
         for i in range(2):
-            nc.scalar.copy(out=r_all[:, halves[i]], in_=r_psum[i][:])
-        nc.scalar.activation(out=norm_all[:], in_=r_all[:], func=ACT.Square)
-        nc.scalar.activation(out=norm_all[:], in_=norm_all[:], func=ACT.Copy, scale=-1.0, bias=1.0)
-        nc.scalar.activation(out=g_all[:], in_=sin_half[:], func=ACT.Square)
-        nc.scalar.activation(out=g_all[:], in_=g_all[:], func=ACT.Copy, scale=-2.0, bias=1.0)
+            nc.vector.tensor_tensor(out=g_all[:, halves[i]], in0=g_all[:, halves[i]], in1=r_psum[i][:],
+                                    op=ALU.mult)
         nc.vector.tensor_scalar(out=root[:], in0=norm_all[:], scalar1=tiny[:, 0:1], scalar2=None, op0=ALU.max)
         nc.scalar.activation(out=root[:], in_=root[:], func=ACT.Sqrt)
         nc.vector.tensor_tensor(out=phi_all[:], in0=phi_all[:], in1=sin_half[:], op=ALU.mult)
-        nc.vector.tensor_tensor(out=phi_all[:], in0=phi_all[:], in1=r_all[:], op=ALU.mult)
-        nc.vector.tensor_tensor(out=g_all[:], in0=g_all[:], in1=r_all[:], op=ALU.mult)
 
         result = [row_tile("result0", "f"), row_tile("result1", "g")]
         nc.vector.tensor_tensor(out=result[0][:], in0=h_sb[0][:], in1=g_all[:], op=ALU.mult)

@@ -21,7 +21,7 @@ SHARE = 4
 N_SETS = (N_PASS + SHARE - 1) // SHARE
 W_BUFS = 13
 AHEAD = 8
-LAST = 3
+HALF = H // 2
 TINY = 1e-30
 FLOPS = 2 * P * D * 2 * H
 
@@ -174,8 +174,8 @@ def tile_linearrtus_w_kernel(
         relu = [row_tile("relu0", "c"), row_tile("relu1", "d")]
 
         loads = [(0, g, 1, 0, H) for g in range(N_PASS)]
-        loads += [(1, g, 1, 0, H) for g in range(N_PASS - LAST)]
-        loads += [(1, N_PASS - LAST, LAST, c, BANK) for c in range(0, H, BANK)]
+        loads += [(1, g, 1, 0, H) for g in range(N_PASS - 1)]
+        loads += [(1, N_PASS - 1, 1, c, HALF) for c in range(0, H, HALF)]
         w_tiles = []
         sums = {}
 
@@ -204,11 +204,13 @@ def tile_linearrtus_w_kernel(
                         stop=(g == N_PASS - 1),
                     )
 
-        def finish(w, c):
-            at = slice(c, c + BANK)
-            nc.vector.tensor_tensor(out=scaled[:, at], in0=sums[(w, c)][:], in1=norm_all[:, at], op=ALU.mult)
-            nc.vector.tensor_tensor(out=result[w][:, at], in0=result[w][:, at], in1=scaled[:, at], op=ALU.add)
-            nc.scalar.activation(out=relu[w][:, at], in_=result[w][:, at], func=ACT.Relu)
+        def finish(w, c0, cols):
+            banks = [slice(c, c + BANK) for c in range(c0, c0 + cols, BANK)]
+            for at in banks:
+                nc.vector.tensor_tensor(out=scaled[:, at], in0=sums[(w, at.start)][:], in1=norm_all[:, at], op=ALU.mult)
+            for at in banks:
+                nc.vector.tensor_tensor(out=result[w][:, at], in0=result[w][:, at], in1=scaled[:, at], op=ALU.add)
+                nc.scalar.activation(out=relu[w][:, at], in_=result[w][:, at], func=ACT.Relu)
 
         def store(w, c0, cols):
             nc.sync.dma_start(out=outs[w][:, c0:c0 + cols], in_=result[w][:, c0:c0 + cols])
@@ -220,8 +222,7 @@ def tile_linearrtus_w_kernel(
             w, g0, n, c0, cols = loads[i]
             multiply(w, g0, n, c0, cols, w_tiles[i])
             if g0 + n == N_PASS:
-                for c in range(c0, c0 + cols, BANK):
-                    finish(w, c)
+                finish(w, c0, cols)
                 if w == 1:
                     store(1, c0, cols)
             if i + AHEAD < len(loads):

@@ -22,6 +22,7 @@ N_SETS = (N_PASS + SHARE - 1) // SHARE
 W_BUFS = 13
 AHEAD = 8
 HALF = H // 2
+DMA_ALIGN = 256
 TINY = 1e-30
 FLOPS = 2 * P * D * 2 * H
 
@@ -41,13 +42,13 @@ def tile_linearrtus_w_kernel(
         ctx.enter_context(tc.manual_schedule())
 
         def row_tile(name, tag):
-            return keep.tile([P, H], F32, name=name, tag=tag)
+            return keep.tile([P, H], F32, name=name, tag=tag, align_bytes=DMA_ALIGN)
 
         def bank_tile(i, shape, dtype, name):
             return psum.tile(shape, dtype, name=name, tag="bank%d" % i)
 
-        x_sb = keep.tile([P, D], BF16, name="x_sb")
-        h_sb = [keep.tile([P, H], BF16, name="h_sb%d" % i) for i in range(2)]
+        x_sb = keep.tile([P, D], BF16, name="x_sb", align_bytes=DMA_ALIGN)
+        h_sb = [keep.tile([P, H], BF16, name="h_sb%d" % i, align_bytes=DMA_ALIGN) for i in range(2)]
         nc.sync.dma_start(out=x_sb[:], in_=x_t[:, :])
         nc.sync.dma_start(out=h_sb[0][:], in_=h_c1[:, :])
         nc.sync.dma_start(out=h_sb[1][:], in_=h_c2[:, :])
@@ -55,7 +56,7 @@ def tile_linearrtus_w_kernel(
         ident = keep.tile([P, P], F32, name="ident")
         make_identity(nc, ident[:])
 
-        planes = keep.tile([P, 2 * N_SETS, H], U8, name="planes", align_bytes=64)
+        planes = keep.tile([P, 2 * N_SETS, H], U8, name="planes", align_bytes=DMA_ALIGN)
         tiny = keep.tile([P, 1], F32, name="tiny")
 
         def load_scale_rows(w, s):
@@ -180,7 +181,7 @@ def tile_linearrtus_w_kernel(
         sums = {}
 
         def load(w, g0, n, c0, cols):
-            wt = wpool.tile([P, H], U32, name="wt", tag="wt", align_bytes=64)
+            wt = wpool.tile([P, H], U32, name="wt", tag="wt", align_bytes=DMA_ALIGN)
             nc.sync.dma_start(
                 out=wt[:, 0:n * cols].rearrange("p (g c) -> p g c", g=n).bitcast(I32),
                 in_=w_words[w][g0:g0 + n].rearrange("g p c t -> p g (c t)")[:, :, 4 * c0:4 * (c0 + cols)].bitcast(I32),

from contextlib import ExitStack

import concourse.mybir as mybir
from concourse.masks import make_identity

FP8X4 = mybir.dt.float8_e4m3fn_x4
BF16 = mybir.dt.bfloat16
F32 = mybir.dt.float32
I32 = mybir.dt.int32
U32 = mybir.dt.uint32
U8 = mybir.dt.uint8
ALU = mybir.AluOpType
ACT = mybir.ActivationFunctionType

P = 128
D, H = 5632, 2048
K_PASS = 512
N_PASS = D // K_PASS
BANK = 512
SHARE = 4
N_SETS = (N_PASS + SHARE - 1) // SHARE
W_BUFS = 13
AHEAD = 8
HALF = H // 2
DMA_ALIGN = 256
TINY = 1e-30
FLOPS = 2 * P * D * 2 * H


def tile_linearrtus_w_kernel(
    tc, h_c1, h_c2, x_t, r_param, theta_param,
    w1_words, w1_scales, w2_words, w2_scales, out_0, out_1, out_2,
):
    nc = tc.nc
    w_words = (w1_words, w2_words)
    w_scales = (w1_scales, w2_scales)
    outs = (out_0, out_1)
    with ExitStack() as ctx:
        keep = ctx.enter_context(tc.tile_pool(name="keep", bufs=1))
        wpool = ctx.enter_context(tc.tile_pool(name="wpool", bufs=W_BUFS))
        psum = ctx.enter_context(tc.psum_pool(name="psum", bufs=1))
        ctx.enter_context(tc.manual_schedule())

        def row_tile(name, tag):
            return keep.tile([P, H], F32, name=name, tag=tag, align_bytes=DMA_ALIGN)

        def bank_tile(i, shape, dtype, name):
            return psum.tile(shape, dtype, name=name, tag="bank%d" % i)

        x_sb = keep.tile([P, D], BF16, name="x_sb", align_bytes=DMA_ALIGN)
        h_sb = [keep.tile([P, H], BF16, name="h_sb%d" % i, align_bytes=DMA_ALIGN) for i in range(2)]
        nc.sync.dma_start(out=x_sb[:], in_=x_t[:, :])
        nc.sync.dma_start(out=h_sb[0][:], in_=h_c1[:, :])
        nc.sync.dma_start(out=h_sb[1][:], in_=h_c2[:, :])

        ident = keep.tile([P, P], F32, name="ident")
        make_identity(nc, ident[:])

        planes = keep.tile([P, 2 * N_SETS, H], U8, name="planes", align_bytes=DMA_ALIGN)
        tiny = keep.tile([P, 1], F32, name="tiny")

        def load_scale_rows(w, s):
            n = min(SHARE, N_PASS - SHARE * s)
            t = N_SETS * w + s
            nc.vector.memset(planes[:, t, :].bitcast(I32), 0)
            for quadrant in range(4):
                nc.gpsimd.dma_start(
                    out=planes[32 * quadrant:32 * quadrant + 4 * n, t, :].bitcast(F32),
                    in_=w_scales[w][SHARE * s:SHARE * s + n, 4 * quadrant:4 * quadrant + 4, :].bitcast(F32),
                )

        for w in range(2):
            for s in range(N_SETS):
                load_scale_rows(w, s)
        nc.gpsimd.memset(tiny[:], TINY)

        vec_rows = keep.tile([P, 2 * H], BF16, name="vec_rows")
        ones = keep.tile([P, P], BF16, name="ones")
        nc.vector.memset(vec_rows[:].bitcast(I32), 0)
        nc.vector.memset(ones[:], 1.0)
        nc.scalar.dma_start(out=vec_rows[0:1, 0:H], in_=theta_param[:, :])
        nc.scalar.dma_start(out=vec_rows[0:1, H:2 * H], in_=r_param[:, :])

        x_words = x_sb[:].bitcast(F32)
        x_grouped = keep.tile([P, N_PASS * K_PASS], BF16, name="x_grouped", align_bytes=64)
        x_grouped_words = x_grouped[:].bitcast(F32).rearrange("p (g b u) -> p g b u", g=N_PASS, b=P, u=2)
        x_codes = keep.tile([P, N_PASS * P], U32, name="x_codes", align_bytes=64)
        x_scales = keep.tile([P, N_PASS * P], U8, name="x_scales", align_bytes=64)
        n_pairs = (N_PASS + 1) // 2
        transposed = []

        def passes_of(pair):
            return range(2 * pair, min(2 * pair + 2, N_PASS))

        def transpose_pair(pair):
            xt = bank_tile(pair % 4, [P, 2, 2, P], F32, "xt%d" % pair)
            for g in passes_of(pair):
                for u in range(2):
                    nc.tensor.transpose(out=xt[:, g % 2, u, :], in_=x_words[:, 256 * g + u:256 * (g + 1):2],
                                        identity=ident[:])
            transposed.append(xt)

        def regroup_pair(pair):
            n = len(passes_of(pair))
            nc.vector.tensor_copy(out=x_grouped_words[:, 2 * pair:2 * pair + n, :, :],
                                  in_=transposed[pair][:, 0:n, :, :].rearrange("p g u b -> p g b u"))

        def quantise_pair(pair):
            n = len(passes_of(pair))
            nc.vector.quantize_mx(
                out=x_codes[:, 2 * P * pair:2 * P * pair + P * n].bitcast(FP8X4),
                scales=x_scales[:, 2 * P * pair:2 * P * pair + P * n],
                in_=x_grouped[:, 2 * K_PASS * pair:2 * K_PASS * pair + K_PASS * n],
            )

        def spread(i):
            out = bank_tile(4 + i, [P, 2 * BANK], BF16, "spread%d" % i)
            for j in range(2):
                c = 2 * BANK * i + BANK * j
                nc.tensor.matmul(out=out[:, BANK * j:BANK * (j + 1)], lhsT=ones[:], rhs=vec_rows[:, c:c + BANK],
                                 start=True, stop=True)
            return out

        for pair in range(4):
            transpose_pair(pair)
        theta_all = [spread(0), spread(1)]
        r_psum = [spread(2), spread(3)]
        for pair in range(n_pairs):
            regroup_pair(pair)
            if pair + 4 < n_pairs:
                transpose_pair(pair + 4)
            if pair > 0:
                quantise_pair(pair - 1)
        quantise_pair(n_pairs - 1)

        halves = (slice(0, H // 2), slice(H // 2, H))
        sin_half = row_tile("sin_half", "a")
        root = row_tile("root", "b")
        g_all = row_tile("g_all", "c")
        phi_all = row_tile("phi_all", "d")
        norm_all = row_tile("norm_all", "e")
        for i in range(2):
            nc.scalar.activation(out=norm_all[:, halves[i]], in_=r_psum[i][:], func=ACT.Square)
        nc.scalar.activation(out=norm_all[:], in_=norm_all[:], func=ACT.Copy, scale=-1.0, bias=1.0)
        for i in range(2):
            nc.scalar.activation(out=sin_half[:, halves[i]], in_=theta_all[i][:], func=ACT.Sin, scale=0.5)
        nc.scalar.activation(out=g_all[:], in_=sin_half[:], func=ACT.Square)
        nc.scalar.activation(out=g_all[:], in_=g_all[:], func=ACT.Copy, scale=-2.0, bias=1.0)
        for i in range(2):
            nc.scalar.activation(out=phi_all[:, halves[i]], in_=theta_all[i][:], func=ACT.Sin, scale=0.25)
        nc.scalar.activation(out=phi_all[:], in_=phi_all[:], func=ACT.Square)
        nc.scalar.activation(out=phi_all[:], in_=phi_all[:], func=ACT.Copy, scale=-4.0, bias=2.0)
        for i in range(2):
            nc.vector.tensor_tensor(out=sin_half[:, halves[i]], in0=sin_half[:, halves[i]], in1=r_psum[i][:],
                                    op=ALU.mult)
        for i in range(2):
            nc.vector.tensor_tensor(out=g_all[:, halves[i]], in0=g_all[:, halves[i]], in1=r_psum[i][:],
                                    op=ALU.mult)
        nc.vector.tensor_scalar(out=root[:], in0=norm_all[:], scalar1=tiny[:, 0:1], scalar2=None, op0=ALU.max)
        nc.scalar.activation(out=root[:], in_=root[:], func=ACT.Sqrt)
        nc.vector.tensor_tensor(out=phi_all[:], in0=phi_all[:], in1=sin_half[:], op=ALU.mult)

        result = [row_tile("result0", "f"), row_tile("result1", "g")]
        nc.vector.tensor_tensor(out=result[0][:], in0=h_sb[0][:], in1=g_all[:], op=ALU.mult)
        cross0 = row_tile("cross0", "a")
        nc.vector.tensor_tensor(out=cross0[:], in0=h_sb[1][:], in1=phi_all[:], op=ALU.mult)
        nc.vector.scalar_tensor_tensor(out=norm_all[:], in0=norm_all[:], scalar=0.0, in1=root[:],
                                       op0=ALU.is_gt, op1=ALU.mult)
        nc.vector.tensor_tensor(out=result[1][:], in0=h_sb[1][:], in1=g_all[:], op=ALU.mult)
        cross1 = row_tile("cross1", "b")
        nc.vector.tensor_tensor(out=cross1[:], in0=h_sb[0][:], in1=phi_all[:], op=ALU.mult)
        nc.vector.tensor_tensor(out=result[0][:], in0=result[0][:], in1=cross0[:], op=ALU.subtract)
        nc.vector.tensor_tensor(out=result[1][:], in0=result[1][:], in1=cross1[:], op=ALU.add)
        scaled = row_tile("scaled", "a")
        relu = [row_tile("relu0", "c"), row_tile("relu1", "d")]

        loads = [(0, g, 1, 0, H) for g in range(N_PASS)]
        loads += [(1, g, 1, 0, H) for g in range(N_PASS - 1)]
        loads += [(1, N_PASS - 1, 1, c, HALF) for c in range(0, H, HALF)]
        w_tiles = []
        sums = {}

        def load(w, g0, n, c0, cols):
            wt = wpool.tile([P, H], U32, name="wt", tag="wt", align_bytes=DMA_ALIGN)
            nc.sync.dma_start(
                out=wt[:, 0:n * cols].rearrange("p (g c) -> p g c", g=n).bitcast(I32),
                in_=w_words[w][g0:g0 + n].rearrange("g p c t -> p g (c t)")[:, :, 4 * c0:4 * (c0 + cols)].bitcast(I32),
            )
            w_tiles.append(wt)

        def multiply(w, g0, n, c0, cols, wt):
            for g in range(g0, g0 + n):
                for c in range(c0, c0 + cols, BANK):
                    if g == 0:
                        b = 4 * w + c // BANK
                        sums[(w, c)] = bank_tile(b, [P, BANK], F32, "sum%d" % b)
                    at = (g - g0) * cols + c - c0
                    nc.tensor.matmul_mx(
                        out=sums[(w, c)][:],
                        lhsT=x_codes[:, P * g:P * (g + 1)].bitcast(FP8X4),
                        lhsT_scale=x_scales[:, P * g:P * (g + 1)],
                        rhs=wt[:, at:at + BANK].bitcast(FP8X4),
                        rhs_scale=planes[4 * (g % SHARE):P, N_SETS * w + g // SHARE, c:c + BANK],
                        start=(g == 0),
                        stop=(g == N_PASS - 1),
                    )

        def finish(w, c0, cols):
            banks = [slice(c, c + BANK) for c in range(c0, c0 + cols, BANK)]
            for at in banks:
                nc.vector.tensor_tensor(out=scaled[:, at], in0=sums[(w, at.start)][:], in1=norm_all[:, at], op=ALU.mult)
            for at in banks:
                nc.vector.tensor_tensor(out=result[w][:, at], in0=result[w][:, at], in1=scaled[:, at], op=ALU.add)
                nc.scalar.activation(out=relu[w][:, at], in_=result[w][:, at], func=ACT.Relu)

        def store(w, c0, cols):
            nc.sync.dma_start(out=outs[w][:, c0:c0 + cols], in_=result[w][:, c0:c0 + cols])
            nc.sync.dma_start(out=out_2[:, H * w + c0:H * w + c0 + cols], in_=relu[w][:, c0:c0 + cols])

        for i in range(AHEAD):
            load(*loads[i])
        for i in range(len(loads)):
            w, g0, n, c0, cols = loads[i]
            multiply(w, g0, n, c0, cols, w_tiles[i])
            if g0 + n == N_PASS:
                finish(w, c0, cols)
                if w == 1:
                    store(1, c0, cols)
            if i + AHEAD < len(loads):
                load(*loads[i + AHEAD])
            if i + AHEAD == len(loads) - 1:
                store(0, 0, H)
